import numpy as np
import ml_dtypes

BF16 = ml_dtypes.bfloat16


def bf(x):
    return np.asarray(x, np.float32).astype(BF16)


def f32(x):
    return np.asarray(x, np.float32)


def f64(x):
    return np.asarray(x).astype(np.float64)


def striped(idx):
    return np.tile(idx.reshape(-1, 16).T, (8, 1))


E, H, M, S, N = 128, 128, 384, 2048, 512


def sigmoid(v):
    return 1.0 / (1.0 + np.exp(-v))


def cell(e, w, b):
    u = f64(w).T @ f64(e) + f64(b)
    state = sigmoid(u[:H]) * np.tanh(u[H:M - H])
    return sigmoid(u[M - H:]) * np.tanh(state)


def setup_inputs():
    return {"base": f32(0.3 * np.random.standard_normal((H, S))), "e": bf(np.random.standard_normal((E, N))), "w_f": bf(np.random.standard_normal((E, M)) / np.sqrt(E)), "b_f": f32(0.5 * np.random.standard_normal((M, 1))), "w_b": bf(np.random.standard_normal((E, M)) / np.sqrt(E)), "b_b": f32(0.5 * np.random.standard_normal((M, 1))), "offs": striped(np.random.permutation(S)[:N])}


def reference(base, e, w_f, b_f, w_b, b_b, offs):
    idx = offs[:16].T.reshape(-1)
    out = f64(base).copy()
    out[:, idx] = cell(e, w_f, b_f) + cell(e, w_b, b_b)
    return out

@@ -1,0 +1,56 @@
+import concourse.mybir as mybir
+
+F32 = mybir.dt.float32
+BF16 = mybir.dt.bfloat16
+U16 = mybir.dt.uint16
+SIGMOID = mybir.ActivationFunctionType.Sigmoid
+TANH = mybir.ActivationFunctionType.Tanh
+MULT = mybir.AluOpType.mult
+ADD = mybir.AluOpType.add
+
+P = 128
+TOKENS = 512
+PLACES = 2048
+GATES = 3
+
+FLOPS = 2 * 2 * P * GATES * P * TOKENS
+
+
+def tile_encoder_multi_kernel(tc, base, e, w_f, b_f, w_b, b_b, offs, out):
+    nc = tc.nc
+    with (
+        tc.tile_pool(name="held", bufs=1) as held,
+        tc.psum_pool(name="psum", bufs=1) as psum,
+    ):
+        tokens = held.tile([P, TOKENS], BF16, name="tokens")
+        nc.sync.dma_start(tokens[:], e)
+        weights = {}
+        biases = {}
+        for d, w, b in (("f", w_f, b_f), ("b", w_b, b_b)):
+            weights[d] = held.tile([P, GATES * P], BF16, name=f"weights_{d}")
+            nc.sync.dma_start(weights[d][:], w)
+            biases[d] = held.tile([P, GATES], F32, name=f"biases_{d}")
+            with nc.allow_non_contiguous_dma(reason="384 biases, one float32 to a partition and gate"):
+                nc.sync.dma_start(biases[d][:], b.rearrange("(g c) one -> c (g one)", c=P))
+        offsets = held.tile([P, TOKENS // 16], U16, name="offsets")
+        nc.sync.dma_start(offsets[:], offs)
+        window = held.tile([P, PLACES], F32, name="window")
+        nc.sync.dma_start(window[:], base)
+
+        hidden = {}
+        for d in ("f", "b"):
+            gate = []
+            for g, func in enumerate((SIGMOID, TANH, SIGMOID)):
+                u = psum.tile([P, TOKENS], F32, name=f"u_{d}{g}")
+                nc.tensor.matmul(u[:], weights[d][:, g * P : (g + 1) * P], tokens[:], start=True, stop=True)
+                gate.append(held.tile([P, TOKENS], F32, name=f"gate_{d}{g}"))
+                nc.scalar.activation(gate[g][:], u[:], func, bias=biases[d][:, g : g + 1])
+            state = held.tile([P, TOKENS], F32, name=f"state_{d}")
+            nc.vector.tensor_tensor(state[:], gate[0][:], gate[1][:], MULT)
+            squashed = held.tile([P, TOKENS], F32, name=f"squashed_{d}")
+            nc.scalar.activation(squashed[:], state[:], TANH)
+            hidden[d] = held.tile([P, TOKENS], F32, name=f"hidden_{d}")
+            nc.vector.tensor_tensor(hidden[d][:], gate[2][:], squashed[:], MULT)
+
+        nc.vector.tensor_tensor(window[:].indirect(offsets[:]), hidden["f"][:], hidden["b"][:], ADD)
+        nc.sync.dma_start(out, window[:])

@@ -22,6 +22,10 @@ def tile_encoder_multi_kernel(tc, base, e, w_f, b_f, w_b, b_b, offs, out):
         tc.tile_pool(name="held", bufs=1) as held,
         tc.psum_pool(name="psum", bufs=1) as psum,
     ):
+        warm = held.tile([P, 1], F32, name="warm")
+        nc.vector.memset(warm[:], 0.0)
+        nc.scalar.activation(warm[:], warm[:], SIGMOID)
+
         tokens = held.tile([P, TOKENS], BF16, name="tokens")
         nc.sync.dma_start(tokens[:], e)
         weights = {}

@@ -22,24 +22,23 @@ def tile_encoder_multi_kernel(tc, base, e, w_f, b_f, w_b, b_b, offs, out):
         tc.tile_pool(name="held", bufs=1) as held,
         tc.psum_pool(name="psum", bufs=1) as psum,
     ):
+        tokens = held.tile([P, TOKENS], BF16, name="tokens")
+        weights = {d: held.tile([P, GATES * P], BF16, name=f"weights_{d}") for d in ("f", "b")}
+        biases = {d: held.tile([P, GATES], F32, name=f"biases_{d}") for d in ("f", "b")}
+        offsets = held.tile([P, TOKENS // 16], U16, name="offsets")
+        window = held.tile([P, PLACES], F32, name="window")
+        nc.sync.dma_start(tokens[:], e)
+        nc.scalar.dma_start(weights["f"][:], w_f)
+        with nc.allow_non_contiguous_dma(reason="384 biases, one float32 to a partition and gate"):
+            nc.scalar.dma_start(biases["f"][:], b_f.rearrange("(g c) one -> c (g one)", c=P))
+            nc.scalar.dma_start(biases["b"][:], b_b.rearrange("(g c) one -> c (g one)", c=P))
+        nc.sync.dma_start(weights["b"][:], w_b)
+        nc.sync.dma_start(offsets[:], offs)
+        nc.sync.dma_start(window[:], base)
+
         warm = held.tile([P, 1], F32, name="warm")
         nc.vector.memset(warm[:], 0.0)
         nc.scalar.activation(warm[:], warm[:], SIGMOID)
-
-        tokens = held.tile([P, TOKENS], BF16, name="tokens")
-        nc.sync.dma_start(tokens[:], e)
-        weights = {}
-        biases = {}
-        for d, w, b in (("f", w_f, b_f), ("b", w_b, b_b)):
-            weights[d] = held.tile([P, GATES * P], BF16, name=f"weights_{d}")
-            nc.sync.dma_start(weights[d][:], w)
-            biases[d] = held.tile([P, GATES], F32, name=f"biases_{d}")
-            with nc.allow_non_contiguous_dma(reason="384 biases, one float32 to a partition and gate"):
-                nc.sync.dma_start(biases[d][:], b.rearrange("(g c) one -> c (g one)", c=P))
-        offsets = held.tile([P, TOKENS // 16], U16, name="offsets")
-        nc.sync.dma_start(offsets[:], offs)
-        window = held.tile([P, PLACES], F32, name="window")
-        nc.sync.dma_start(window[:], base)
 
         hidden = {}
         for d in ("f", "b"):

@@ -13,6 +13,9 @@ TOKENS = 512
 PLACES = 2048
 GATES = 3
 
+WHOLE = ((0, TOKENS),)
+HALVES = ((0, TOKENS // 2), (TOKENS // 2, TOKENS))
+
 FLOPS = 2 * 2 * P * GATES * P * TOKENS
 
 
@@ -22,38 +25,41 @@ def tile_encoder_multi_kernel(tc, base, e, w_f, b_f, w_b, b_b, offs, out):
         tc.tile_pool(name="held", bufs=1) as held,
         tc.psum_pool(name="psum", bufs=1) as psum,
     ):
-        tokens = held.tile([P, TOKENS], BF16, name="tokens")
-        weights = {d: held.tile([P, GATES * P], BF16, name=f"weights_{d}") for d in ("f", "b")}
-        biases = {d: held.tile([P, GATES], F32, name=f"biases_{d}") for d in ("f", "b")}
-        offsets = held.tile([P, TOKENS // 16], U16, name="offsets")
-        window = held.tile([P, PLACES], F32, name="window")
-        nc.sync.dma_start(tokens[:], e)
-        nc.scalar.dma_start(weights["f"][:], w_f)
-        with nc.allow_non_contiguous_dma(reason="384 biases, one float32 to a partition and gate"):
-            nc.scalar.dma_start(biases["f"][:], b_f.rearrange("(g c) one -> c (g one)", c=P))
-            nc.scalar.dma_start(biases["b"][:], b_b.rearrange("(g c) one -> c (g one)", c=P))
-        nc.sync.dma_start(weights["b"][:], w_b)
-        nc.sync.dma_start(offsets[:], offs)
-        nc.sync.dma_start(window[:], base)
-
         warm = held.tile([P, 1], F32, name="warm")
         nc.vector.memset(warm[:], 0.0)
         nc.scalar.activation(warm[:], warm[:], SIGMOID)
+
+        tokens = held.tile([P, TOKENS], BF16, name="tokens")
+        nc.sync.dma_start(tokens[:], e)
+        weights = {}
+        biases = {}
+        for d, w, b in (("f", w_f, b_f), ("b", w_b, b_b)):
+            weights[d] = held.tile([P, GATES * P], BF16, name=f"weights_{d}")
+            nc.sync.dma_start(weights[d][:], w)
+            biases[d] = held.tile([P, GATES], F32, name=f"biases_{d}")
+            with nc.allow_non_contiguous_dma(reason="384 biases, one float32 to a partition and gate"):
+                nc.sync.dma_start(biases[d][:], b.rearrange("(g c) one -> c (g one)", c=P))
+        offsets = held.tile([P, TOKENS // 16], U16, name="offsets")
+        nc.sync.dma_start(offsets[:], offs)
+        window = held.tile([P, PLACES], F32, name="window")
+        nc.sync.dma_start(window[:], base)
 
         hidden = {}
         for d in ("f", "b"):
             gate = []
             for g, func in enumerate((SIGMOID, TANH, SIGMOID)):
-                u = psum.tile([P, TOKENS], F32, name=f"u_{d}{g}")
-                nc.tensor.matmul(u[:], weights[d][:, g * P : (g + 1) * P], tokens[:], start=True, stop=True)
                 gate.append(held.tile([P, TOKENS], F32, name=f"gate_{d}{g}"))
-                nc.scalar.activation(gate[g][:], u[:], func, bias=biases[d][:, g : g + 1])
+                for lo, hi in HALVES if (d, g) == ("f", 0) else WHOLE:
+                    u = psum.tile([P, hi - lo], F32, name=f"u_{d}{g}_{lo}")
+                    nc.tensor.matmul(u[:], weights[d][:, g * P : (g + 1) * P], tokens[:, lo:hi], start=True, stop=True)
+                    nc.scalar.activation(gate[g][:, lo:hi], u[:], func, bias=biases[d][:, g : g + 1])
             state = held.tile([P, TOKENS], F32, name=f"state_{d}")
             nc.vector.tensor_tensor(state[:], gate[0][:], gate[1][:], MULT)
             squashed = held.tile([P, TOKENS], F32, name=f"squashed_{d}")
-            nc.scalar.activation(squashed[:], state[:], TANH)
             hidden[d] = held.tile([P, TOKENS], F32, name=f"hidden_{d}")
-            nc.vector.tensor_tensor(hidden[d][:], gate[2][:], squashed[:], MULT)
+            for lo, hi in HALVES if d == "b" else WHOLE:
+                nc.scalar.activation(squashed[:, lo:hi], state[:, lo:hi], TANH)
+                nc.vector.tensor_tensor(hidden[d][:, lo:hi], gate[2][:, lo:hi], squashed[:, lo:hi], MULT)
 
         nc.vector.tensor_tensor(window[:].indirect(offsets[:]), hidden["f"][:], hidden["b"][:], ADD)
         nc.sync.dma_start(out, window[:])

@@ -15,6 +15,7 @@ GATES = 3
 
 WHOLE = ((0, TOKENS),)
 HALVES = ((0, TOKENS // 2), (TOKENS // 2, TOKENS))
+QUARTERS = tuple((lo, lo + TOKENS // 4) for lo in range(0, TOKENS, TOKENS // 4))
 
 FLOPS = 2 * 2 * P * GATES * P * TOKENS
 
@@ -30,12 +31,13 @@ def tile_encoder_multi_kernel(tc, base, e, w_f, b_f, w_b, b_b, offs, out):
         nc.scalar.activation(warm[:], warm[:], SIGMOID)
 
         tokens = held.tile([P, TOKENS], BF16, name="tokens")
-        nc.sync.dma_start(tokens[:], e)
         weights = {}
         biases = {}
         for d, w, b in (("f", w_f, b_f), ("b", w_b, b_b)):
             weights[d] = held.tile([P, GATES * P], BF16, name=f"weights_{d}")
             nc.sync.dma_start(weights[d][:], w)
+            if d == "f":
+                nc.sync.dma_start(tokens[:], e)
             biases[d] = held.tile([P, GATES], F32, name=f"biases_{d}")
             with nc.allow_non_contiguous_dma(reason="384 biases, one float32 to a partition and gate"):
                 nc.sync.dma_start(biases[d][:], b.rearrange("(g c) one -> c (g one)", c=P))
@@ -53,11 +55,13 @@ def tile_encoder_multi_kernel(tc, base, e, w_f, b_f, w_b, b_b, offs, out):
                     u = psum.tile([P, hi - lo], F32, name=f"u_{d}{g}_{lo}")
                     nc.tensor.matmul(u[:], weights[d][:, g * P : (g + 1) * P], tokens[:, lo:hi], start=True, stop=True)
                     nc.scalar.activation(gate[g][:, lo:hi], u[:], func, bias=biases[d][:, g : g + 1])
+            pieces = QUARTERS if d == "b" else WHOLE
             state = held.tile([P, TOKENS], F32, name=f"state_{d}")
-            nc.vector.tensor_tensor(state[:], gate[0][:], gate[1][:], MULT)
+            for lo, hi in pieces:
+                nc.vector.tensor_tensor(state[:, lo:hi], gate[0][:, lo:hi], gate[1][:, lo:hi], MULT)
             squashed = held.tile([P, TOKENS], F32, name=f"squashed_{d}")
             hidden[d] = held.tile([P, TOKENS], F32, name=f"hidden_{d}")
-            for lo, hi in HALVES if d == "b" else WHOLE:
+            for lo, hi in pieces:
                 nc.scalar.activation(squashed[:, lo:hi], state[:, lo:hi], TANH)
                 nc.vector.tensor_tensor(hidden[d][:, lo:hi], gate[2][:, lo:hi], squashed[:, lo:hi], MULT)
 

@@ -12,6 +12,7 @@ P = 128
 TOKENS = 512
 PLACES = 2048
 GATES = 3
+BLOCK = 8
 
 WHOLE = ((0, TOKENS),)
 HALVES = ((0, TOKENS // 2), (TOKENS // 2, TOKENS))
@@ -38,9 +39,12 @@ def tile_encoder_multi_kernel(tc, base, e, w_f, b_f, w_b, b_b, offs, out):
             nc.sync.dma_start(weights[d][:], w)
             if d == "f":
                 nc.sync.dma_start(tokens[:], e)
-            biases[d] = held.tile([P, GATES], F32, name=f"biases_{d}")
+            biases[d] = held.tile([P, GATES * BLOCK], F32, name=f"biases_{d}")
             with nc.allow_non_contiguous_dma(reason="384 biases, one float32 to a partition and gate"):
-                nc.sync.dma_start(biases[d][:], b.rearrange("(g c) one -> c (g one)", c=P))
+                nc.sync.dma_start(
+                    biases[d][:].rearrange("c (g block) -> c g block", block=BLOCK)[:, :, 0:1],
+                    b.rearrange("(g c) one -> c g one", c=P),
+                )
         offsets = held.tile([P, TOKENS // 16], U16, name="offsets")
         nc.sync.dma_start(offsets[:], offs)
         window = held.tile([P, PLACES], F32, name="window")
@@ -54,7 +58,7 @@ def tile_encoder_multi_kernel(tc, base, e, w_f, b_f, w_b, b_b, offs, out):
                 for lo, hi in HALVES if (d, g) == ("f", 0) else WHOLE:
                     u = psum.tile([P, hi - lo], F32, name=f"u_{d}{g}_{lo}")
                     nc.tensor.matmul(u[:], weights[d][:, g * P : (g + 1) * P], tokens[:, lo:hi], start=True, stop=True)
-                    nc.scalar.activation(gate[g][:, lo:hi], u[:], func, bias=biases[d][:, g : g + 1])
+                    nc.scalar.activation(gate[g][:, lo:hi], u[:], func, bias=biases[d][:, g * BLOCK : g * BLOCK + 1])
             pieces = QUARTERS if d == "b" else WHOLE
             state = held.tile([P, TOKENS], F32, name=f"state_{d}")
             for lo, hi in pieces:

import concourse.mybir as mybir

F32 = mybir.dt.float32
BF16 = mybir.dt.bfloat16
U16 = mybir.dt.uint16
SIGMOID = mybir.ActivationFunctionType.Sigmoid
TANH = mybir.ActivationFunctionType.Tanh
MULT = mybir.AluOpType.mult
ADD = mybir.AluOpType.add

P = 128
TOKENS = 512
PLACES = 2048
GATES = 3
BLOCK = 8

WHOLE = ((0, TOKENS),)
HALVES = ((0, TOKENS // 2), (TOKENS // 2, TOKENS))
QUARTERS = tuple((lo, lo + TOKENS // 4) for lo in range(0, TOKENS, TOKENS // 4))

FLOPS = 2 * 2 * P * GATES * P * TOKENS


def tile_encoder_multi_kernel(tc, base, e, w_f, b_f, w_b, b_b, offs, out):
    nc = tc.nc
    with (
        tc.tile_pool(name="held", bufs=1) as held,
        tc.psum_pool(name="psum", bufs=1) as psum,
    ):
        warm = held.tile([P, 1], F32, name="warm")
        nc.vector.memset(warm[:], 0.0)
        nc.scalar.activation(warm[:], warm[:], SIGMOID)

        tokens = held.tile([P, TOKENS], BF16, name="tokens")
        weights = {}
        biases = {}
        for d, w, b in (("f", w_f, b_f), ("b", w_b, b_b)):
            weights[d] = held.tile([P, GATES * P], BF16, name=f"weights_{d}")
            nc.sync.dma_start(weights[d][:], w)
            if d == "f":
                nc.sync.dma_start(tokens[:], e)
            biases[d] = held.tile([P, GATES * BLOCK], F32, name=f"biases_{d}")
            with nc.allow_non_contiguous_dma(reason="384 biases, one float32 to a partition and gate"):
                nc.sync.dma_start(
                    biases[d][:].rearrange("c (g block) -> c g block", block=BLOCK)[:, :, 0:1],
                    b.rearrange("(g c) one -> c g one", c=P),
                )
        offsets = held.tile([P, TOKENS // 16], U16, name="offsets")
        nc.sync.dma_start(offsets[:], offs)
        window = held.tile([P, PLACES], F32, name="window")
        nc.sync.dma_start(window[:], base)

        hidden = {}
        for d in ("f", "b"):
            gate = []
            for g, func in enumerate((SIGMOID, TANH, SIGMOID)):
                gate.append(held.tile([P, TOKENS], F32, name=f"gate_{d}{g}"))
                for lo, hi in HALVES if (d, g) == ("f", 0) else WHOLE:
                    u = psum.tile([P, hi - lo], F32, name=f"u_{d}{g}_{lo}")
                    nc.tensor.matmul(u[:], weights[d][:, g * P : (g + 1) * P], tokens[:, lo:hi], start=True, stop=True)
                    nc.scalar.activation(gate[g][:, lo:hi], u[:], func, bias=biases[d][:, g * BLOCK : g * BLOCK + 1])
            pieces = QUARTERS if d == "b" else WHOLE
            state = held.tile([P, TOKENS], F32, name=f"state_{d}")
            for lo, hi in pieces:
                nc.vector.tensor_tensor(state[:, lo:hi], gate[0][:, lo:hi], gate[1][:, lo:hi], MULT)
            squashed = held.tile([P, TOKENS], F32, name=f"squashed_{d}")
            hidden[d] = held.tile([P, TOKENS], F32, name=f"hidden_{d}")
            for lo, hi in pieces:
                nc.scalar.activation(squashed[:, lo:hi], state[:, lo:hi], TANH)
                nc.vector.tensor_tensor(hidden[d][:, lo:hi], gate[2][:, lo:hi], squashed[:, lo:hi], MULT)

        nc.vector.tensor_tensor(window[:].indirect(offsets[:]), hidden["f"][:], hidden["b"][:], ADD)
        nc.sync.dma_start(out, window[:])
